import numpy as np
import ml_dtypes


def mxq(x, axis, fmt="e4m3"):
    dtype, down = {"e4m3": (ml_dtypes.float8_e4m3fn, 7), "e5m2": (ml_dtypes.float8_e5m2, 14)}[fmt]
    v = np.moveaxis(np.asarray(x, np.float32).astype(ml_dtypes.bfloat16).astype(np.float64), axis, -1)
    blocks = v.reshape(v.shape[:-1] + (-1, 32))
    amax = np.abs(blocks).max(-1, keepdims=True)
    byte = np.maximum(np.where(amax > 0, np.frexp(amax)[1] - 1 + 127, 0) - down, 1)
    scale = np.exp2(byte - 127.0)
    codes = (blocks / scale).astype(np.float32).astype(dtype).astype(np.float64)
    return np.moveaxis((codes * scale).reshape(v.shape), -1, axis)


WIDE = False


def mx_kscale(k):
    if not WIDE:
        return np.ones(k)
    levels = np.array([10, -10, 5, -5, 0])
    if k % 512:
        return np.exp2(np.random.permutation(np.resize(levels, k // 32))).repeat(32)
    a = np.empty((k // 512, 16))
    for p in range(k // 512):
        a[p, :8] = np.random.permutation(np.resize(levels, 8))
        for g in range(8):
            far = levels[np.abs(levels - a[p, g]) >= 10]
            a[p, g + 8] = far[np.random.randint(len(far))]
    return np.exp2(a.ravel()).repeat(32)


BF16 = ml_dtypes.bfloat16


def bf(x):
    return np.asarray(x, np.float32).astype(BF16)


def f64(x):
    return np.asarray(x).astype(np.float64)


B, N, DIM, H, DH = 2, 256, 1536, 16, 96
D1 = DH // 3


def rotate_half(t):
    d = t.shape[-1]
    t1, t2 = t[..., : (d + 1) // 2], t[..., (d + 1) // 2:]
    return np.concatenate((-t2, t1), axis=-1)


def apply_rope(t, freqs):
    return t * np.cos(freqs) + rotate_half(t) * np.sin(freqs)


def rope3(t, fs):
    return np.concatenate([apply_rope(ts, f) for ts, f in zip(np.split(t, (D1, 2 * D1), axis=-1), fs)], axis=-1)


def draw0():
    s = mx_kscale(DIM)
    return {"x": bf(np.random.standard_normal((B, N, DIM)) * s),
            "f1": bf(np.random.uniform(0.0, 1.0, (N, D1))),
            "f2": bf(np.random.uniform(0.0, 1.0, (N, D1))),
            "f3": bf(np.random.uniform(0.0, 1.0, (N, D1))),
            "Wqkv": bf(np.random.standard_normal((DIM, 3 * H * DH)) / np.sqrt(DIM) / s[:, None])}


def core(x, f1, f2, f3, Wqkv):
    qkv = mxq(f64(x), 2, "e4m3") @ mxq(f64(Wqkv), 0, "e4m3")
    q, k, v = np.split(qkv, 3, axis=-1)
    to_heads = lambda t: t.reshape(B, N, H, DH).transpose(0, 2, 1, 3)
    q, k, v = to_heads(q), to_heads(k), to_heads(v)
    fs = (f64(f1), f64(f2), f64(f3))
    return rope3(q, fs), rope3(k, fs), v


def e4m3fn_bytes(y):
    return np.clip(np.asarray(y, np.float64), -448.0, 448.0).astype(np.float32).astype(ml_dtypes.float8_e4m3fn).view(np.uint8)


def e4m3fn_values(b):
    return np.asarray(b, np.uint8).view(ml_dtypes.float8_e4m3fn).astype(np.float64)


def setup_inputs():
    d = draw0()
    x0 = np.asarray(d['Wqkv']).astype(np.float64)
    s = (np.max(np.abs(x0), axis=(1,), keepdims=True) / 448.0).astype(np.float32)
    out = {}
    for k, v in d.items():
        if k == 'Wqkv':
            out['Wqkv_bytes'] = e4m3fn_bytes(x0 / s.astype(np.float64))
            out['Wqkv_scale'] = s
        else:
            out[k] = v
    return out


def reference(x, f1, f2, f3, Wqkv_bytes, Wqkv_scale):
    return core(x, f1, f2, f3, e4m3fn_values(Wqkv_bytes) * Wqkv_scale.astype(np.float64))

@@ -1,0 +1,267 @@
+from contextlib import ExitStack
+
+import concourse.mybir as mybir
+from concourse.masks import make_identity
+
+F32 = mybir.dt.float32
+BF16 = mybir.dt.bfloat16
+U32 = mybir.dt.uint32
+U8 = mybir.dt.uint8
+FP8 = mybir.dt.float8_e4m3fn
+FP8X4 = mybir.dt.float8_e4m3fn_x4
+ACT = mybir.ActivationFunctionType
+ALU = mybir.AluOpType
+
+P = 128
+TOK = 512
+DIM = 1536
+COLS = 4608
+HEADS = 16
+DH = 96
+TCOLS = HEADS * DH
+NB = 512
+PASSES = 3
+MT = TOK // P
+TABW = 576
+TILES = tuple((NB * i, NB) for i in range(8)) + ((4096, 256), (4352, 128), (4480, 128))
+NT = len(TILES)
+NCH = NT * PASSES
+ROPED = 6
+
+FLOPS = 2 * TOK * DIM * COLS
+
+VCOLS = (400, 400, 272, 272, 272, 272, 272, 272, 256, 128, 128)
+LAG = 5
+TABLE_STEP = 2
+
+
+def tile_attention_pa_kernel(tc, x, f1, f2, f3, Wqkv_bytes, Wqkv_scale, out_0, out_1, out_2):
+    nc = tc.nc
+    outs = (out_0, out_1, out_2)
+
+    with ExitStack() as ctx:
+        const = ctx.enter_context(tc.tile_pool(name="const", bufs=1))
+        wbp = ctx.enter_context(tc.tile_pool(name="wbytes", bufs=1))
+        stage = ctx.enter_context(tc.tile_pool(name="stage", bufs=4))
+        psum = ctx.enter_context(tc.psum_pool(name="psum", bufs=1))
+        ctx.enter_context(tc.manual_schedule())
+
+        wsc = const.tile([P, PASSES, 4], F32, name="wsc")
+        nc.scalar.dma_start(out=wsc[:], in_=Wqkv_scale.rearrange("(g p t) o -> p g (t o)", p=P, t=4))
+        fsb = const.tile([P, 2, DH], BF16, name="fsb")
+        warm = const.tile([P, 2], F32, name="warm")
+        nc.vector.memset(warm[:], 0.0)
+        nc.scalar.activation(out=warm[:, 1:2], in_=warm[:, 0:1], func=ACT.Sin)
+
+        wview = Wqkv_bytes.rearrange("(g p t) c -> g p t c", p=P, t=4)
+        xf = x.flatten_outer_dims()
+        wb = []
+        x_sb = []
+
+        def load_w(c):
+            n, g = divmod(c, PASSES)
+            c0, wd = TILES[n]
+            t = wbp.tile([P, 4, wd], U8, name="wb%d" % c)
+            nc.sync.dma_start(out=t[:], in_=wview[g][:, :, c0 : c0 + wd])
+            wb.append(t)
+
+        load_w(0)
+        for m in range(MT):
+            t = const.tile([P, DIM], BF16, name="x%d" % m)
+            nc.sync.dma_start(out=t[:], in_=xf[P * m : P * (m + 1), :])
+            x_sb.append(t)
+        for gi, f in enumerate((f1, f2, f3)):
+            nc.sync.dma_start(out=fsb[:, :, 32 * gi : 32 * gi + 32], in_=f.rearrange("(h p) j -> p h j", p=P))
+        for c in range(1, NCH):
+            load_w(c)
+
+        ident = const.tile([P, P], F32, name="ident")
+        make_identity(nc, ident[:])
+
+        cos_t = const.tile([P, 2, TABW], F32, name="cos_t")
+        ssw_t = const.tile([P, 2, TABW], F32, name="ssw_t")
+
+        def tables():
+            sh = const.tile([P, 2, DH], F32, name="sh")
+            nc.scalar.activation(out=sh[:], in_=fsb[:], func=ACT.Sin, scale=0.5)
+            sswb = const.tile([P, 2, DH], F32, name="sswb")
+            fv = fsb[:].rearrange("p h (g e i) -> p (h g) e i", e=2, i=16)
+            sv = sswb[:].rearrange("p h (g e i) -> p (h g) e i", e=2, i=16)
+            nc.scalar.activation(out=sv[:, :, 0, :], in_=fv[:, :, 1, :], func=ACT.Sin)
+            nc.scalar.activation(out=sv[:, :, 1, :], in_=fv[:, :, 0, :], func=ACT.Sin, scale=-1.0)
+            sq = const.tile([P, 2, DH], F32, name="sq")
+            nc.vector.tensor_tensor(out=sq[:], in0=sh[:], in1=sh[:], op=ALU.mult)
+            reps = TABW // DH
+            nc.vector.tensor_copy(
+                out=ssw_t[:].rearrange("p h (r d) -> p h r d", d=DH),
+                in_=sswb[:].unsqueeze(2).to_broadcast([P, 2, reps, DH]),
+            )
+            nc.vector.tensor_scalar(
+                out=cos_t[:].rearrange("p h (r d) -> p h r d", d=DH),
+                in0=sq[:].unsqueeze(2).to_broadcast([P, 2, reps, DH]),
+                scalar1=-2.0,
+                scalar2=1.0,
+                op0=ALU.mult,
+                op1=ALU.add,
+            )
+
+        xc = const.tile([P, PASSES, MT, P], U32, name="xc", align_bytes=64)
+        xs = const.tile([P, PASSES, MT, P], U8, name="xs", align_bytes=64)
+        xgs = {}
+
+        def x_turn(mp, g):
+            xt = psum.tile([P, 2, 2, P], F32, name="xt", tag="bank%d" % (3 * mp + g))
+            for mi in range(2):
+                words = x_sb[2 * mp + mi][:].bitcast(F32)
+                for u in range(2):
+                    nc.tensor.transpose(xt[:, mi, u, :], words[:, 256 * g + u : 256 * (g + 1) : 2], ident[:])
+            xg = stage.tile([P, 2 * P * 4], BF16, name="xg", tag="xg", bufs=3, align_bytes=64)
+            nc.vector.tensor_copy(
+                out=xg[:].bitcast(F32).rearrange("p (m r u) -> p m r u", m=2, u=2),
+                in_=xt[:].rearrange("p m u r -> p m r u"),
+            )
+            xgs[(mp, g)] = xg
+
+        def x_quant(mp, g):
+            nc.vector.quantize_mx(
+                out=xc[:, g, 2 * mp : 2 * mp + 2, :].rearrange("p m r -> p (m r)").bitcast(FP8X4),
+                scales=xs[:, g, 2 * mp : 2 * mp + 2, :].rearrange("p m r -> p (m r)"),
+                in_=xgs[(mp, g)][:],
+            )
+
+        xorder = [(mp, g) for mp in range(2) for g in range(PASSES)]
+        for i, (mp, g) in enumerate(xorder):
+            x_turn(mp, g)
+            if i >= 1:
+                x_quant(*xorder[i - 1])
+        x_quant(*xorder[-1])
+
+        planes = {}
+        inter = {}
+        codes = {}
+        acc = {}
+        prod_c = {}
+        prod_s = {}
+        res = {}
+
+        def widen(c):
+            n, g = divmod(c, PASSES)
+            wd = TILES[n][1]
+            pl = stage.tile([P, 4, wd], BF16, name="pl", tag="pl", bufs=4)
+            for t in range(4):
+                nc.scalar.activation(
+                    out=pl[:, t, :], in_=wb[c][:, t, :].bitcast(FP8), func=ACT.Copy, scale=wsc[:, g, t : t + 1]
+                )
+            planes[c] = pl
+
+        def interleave(c):
+            n = c // PASSES
+            wd = TILES[n][1]
+            vc = VCOLS[n]
+            pl = planes[c]
+            il = stage.tile([P, wd, 4], BF16, name="il", tag="il", bufs=4, align_bytes=64)
+            if vc > 0:
+                nc.vector.tensor_copy(out=il[:, 0:vc, :], in_=pl[:, :, 0:vc].rearrange("p t c -> p c t"))
+            if vc < wd:
+                nc.scalar.copy(out=il[:, vc:wd, :], in_=pl[:, :, vc:wd].rearrange("p t c -> p c t"))
+            inter[c] = il
+
+        def quantize(c):
+            wd = TILES[c // PASSES][1]
+            wc = stage.tile([P, wd], U32, name="wc", tag="wc", bufs=6, align_bytes=64)
+            ws = stage.tile([P, wd], U8, name="ws", tag="ws", bufs=6, align_bytes=64)
+            nc.vector.quantize_mx(
+                out=wc[:].bitcast(FP8X4), scales=ws[:], in_=inter[c][:].rearrange("p c t -> p (c t)")
+            )
+            codes[c] = (wc, ws)
+
+        def matmuls(c):
+            n, g = divmod(c, PASSES)
+            wd = TILES[n][1]
+            wc, ws = codes[c]
+            for m in range(MT):
+                if g == 0:
+                    acc[(n, m)] = psum.tile([P, wd], F32, name="acc", tag="bank%d" % (4 * (n % 2) + m))
+                nc.tensor.matmul_mx(
+                    out=acc[(n, m)][:],
+                    lhsT=xc[:, g, m, :].bitcast(FP8X4),
+                    lhsT_scale=xs[:, g, m, :],
+                    rhs=wc[:].bitcast(FP8X4),
+                    rhs_scale=ws[:],
+                    start=(g == 0),
+                    stop=(g == PASSES - 1),
+                )
+
+        def result_tile(n):
+            tens, lc = divmod(TILES[n][0], TCOLS)
+            if lc == 0 and tens not in res:
+                res[tens] = stage.tile([P, MT, TCOLS], F32, name="res", tag="res", bufs=2)
+            return res[tens], lc
+
+        def mults(n, m):
+            if m == 0:
+                prod_c[n] = stage.tile([P, MT, NB], F32, name="pc", tag="pc", bufs=2)
+                prod_s[n] = stage.tile([P, MT, NB], F32, name="ps", tag="ps", bufs=2)
+            off = TILES[n][0] % DH
+            th = m % 2
+            nc.vector.tensor_tensor(
+                out=prod_c[n][:, m, :], in0=acc[(n, m)][:], in1=cos_t[:, th, off : off + NB], op=ALU.mult
+            )
+            nc.vector.tensor_tensor(
+                out=prod_s[n][:, m, :], in0=acc[(n, m)][:], in1=ssw_t[:, th, off : off + NB], op=ALU.mult
+            )
+
+        def add_half(n, e):
+            r, lc = result_tile(n)
+            rv = r[:, :, lc : lc + NB].rearrange("p m (g e i) -> p m g e i", e=2, i=16)
+            cv = prod_c[n][:].rearrange("p m (g e i) -> p m g e i", e=2, i=16)
+            sv2 = prod_s[n][:].rearrange("p m (g e i) -> p m g e i", e=2, i=16)
+            nc.vector.tensor_tensor(out=rv[:, :, :, e, :], in0=cv[:, :, :, e, :], in1=sv2[:, :, :, 1 - e, :], op=ALU.add)
+
+        def store(n, m):
+            r, lc = result_tile(n)
+            tens = TILES[n][0] // TCOLS
+            h0 = lc // DH
+            h1 = (lc + TILES[n][1]) // DH
+            b, th = divmod(m, 2)
+            nc.sync.dma_start(
+                out=outs[tens][b, h0:h1, P * th : P * (th + 1), :].rearrange("h n d -> n h d"),
+                in_=r[:, m, DH * h0 : DH * h1].rearrange("p (h d) -> p h d", d=DH),
+            )
+
+        def evac(n, m):
+            r, lc = result_tile(n)
+            wd = TILES[n][1]
+            if m % 2 == 0:
+                nc.scalar.copy(out=r[:, m, lc : lc + wd], in_=acc[(n, m)][:])
+            else:
+                nc.vector.tensor_copy(out=r[:, m, lc : lc + wd], in_=acc[(n, m)][:])
+            store(n, m)
+
+        def post(n, part):
+            if n < ROPED:
+                if part < 4:
+                    mults(n, part)
+                else:
+                    add_half(n, part - 4)
+                    if part == 5:
+                        for m in range(MT):
+                            store(n, m)
+            elif part < 4:
+                evac(n, part)
+
+        for k in range(NCH + LAG + 3):
+            if k < NCH:
+                widen(k)
+            if k == TABLE_STEP:
+                tables()
+            if 0 <= k - 1 < NCH:
+                interleave(k - 1)
+            pn, pstep = divmod(k - LAG, 3)
+            if 0 <= pn < NT:
+                post(pn, 2 * pstep)
+            if 0 <= k - 2 < NCH:
+                quantize(k - 2)
+                matmuls(k - 2)
+            if 0 <= pn < NT:
+                post(pn, 2 * pstep + 1)

@@ -27,11 +27,13 @@ TILES = tuple((NB * i, NB) for i in range(8)) + ((4096, 256), (4352, 128), (4480
 NT = len(TILES)
 NCH = NT * PASSES
 ROPED = 6
+ACC_BANKS = 6
 
 FLOPS = 2 * TOK * DIM * COLS
 
-VCOLS = (400, 400, 272, 272, 272, 272, 272, 272, 256, 128, 128)
-LAG = 5
+VCOLS = (400, 256, 176, 176, 176, 176, 176, 176, 256, 128, 128)
+PCOLS = (0, 256, 256, 256, 256, 256, 256, 256, 0, 0, 0)
+LAG = 6
 TABLE_STEP = 2
 
 
@@ -77,6 +79,8 @@ def tile_attention_pa_kernel(tc, x, f1, f2, f3, Wqkv_bytes, Wqkv_scale, out_0, o
 
         ident = const.tile([P, P], F32, name="ident")
         make_identity(nc, ident[:])
+        identb = const.tile([P, P], BF16, name="identb")
+        make_identity(nc, identb[:])
 
         cos_t = const.tile([P, 2, TABW], F32, name="cos_t")
         ssw_t = const.tile([P, 2, TABW], F32, name="ssw_t")
@@ -110,7 +114,7 @@ def tile_attention_pa_kernel(tc, x, f1, f2, f3, Wqkv_bytes, Wqkv_scale, out_0, o
         xgs = {}
 
         def x_turn(mp, g):
-            xt = psum.tile([P, 2, 2, P], F32, name="xt", tag="bank%d" % (3 * mp + g))
+            xt = psum.tile([P, 2, 2, P], F32, name="xt", tag="acc%d" % (3 * mp + g))
             for mi in range(2):
                 words = x_sb[2 * mp + mi][:].bitcast(F32)
                 for u in range(2):
@@ -154,17 +158,32 @@ def tile_attention_pa_kernel(tc, x, f1, f2, f3, Wqkv_bytes, Wqkv_scale, out_0, o
                 )
             planes[c] = pl
 
-        def interleave(c):
+        def interleave_s(c):
             n = c // PASSES
             wd = TILES[n][1]
             vc = VCOLS[n]
+            pcn = PCOLS[n]
             pl = planes[c]
             il = stage.tile([P, wd, 4], BF16, name="il", tag="il", bufs=4, align_bytes=64)
-            if vc > 0:
-                nc.vector.tensor_copy(out=il[:, 0:vc, :], in_=pl[:, :, 0:vc].rearrange("p t c -> p c t"))
-            if vc < wd:
-                nc.scalar.copy(out=il[:, vc:wd, :], in_=pl[:, :, vc:wd].rearrange("p t c -> p c t"))
             inter[c] = il
+            if pcn > 0:
+                pb = psum.tile([P, 4 * pcn], BF16, name="pb", tag="pb%d" % (c % 2))
+                for c0 in range(0, pcn, P):
+                    w = min(P, pcn - c0)
+                    nc.tensor.matmul(
+                        out=pb[:, 4 * c0 : 4 * (c0 + w)],
+                        lhsT=identb[:],
+                        rhs=pl[:, :, vc + c0 : vc + c0 + w].rearrange("p t c -> p c t"),
+                        start=True,
+                        stop=True,
+                    )
+                nc.scalar.copy(out=il[:, vc : vc + pcn, :].rearrange("p c t -> p (c t)"), in_=pb[:])
+            if vc + pcn < wd:
+                nc.scalar.copy(out=il[:, vc + pcn : wd, :], in_=pl[:, :, vc + pcn : wd].rearrange("p t c -> p c t"))
+
+        def interleave_v(c):
+            vc = VCOLS[c // PASSES]
+            nc.vector.tensor_copy(out=inter[c][:, 0:vc, :], in_=planes[c][:, :, 0:vc].rearrange("p t c -> p c t"))
 
         def quantize(c):
             wd = TILES[c // PASSES][1]
@@ -175,22 +194,21 @@ def tile_attention_pa_kernel(tc, x, f1, f2, f3, Wqkv_bytes, Wqkv_scale, out_0, o
             )
             codes[c] = (wc, ws)
 
-        def matmuls(c):
-            n, g = divmod(c, PASSES)
+        def matmuls(n):
             wd = TILES[n][1]
-            wc, ws = codes[c]
             for m in range(MT):
-                if g == 0:
-                    acc[(n, m)] = psum.tile([P, wd], F32, name="acc", tag="bank%d" % (4 * (n % 2) + m))
-                nc.tensor.matmul_mx(
-                    out=acc[(n, m)][:],
-                    lhsT=xc[:, g, m, :].bitcast(FP8X4),
-                    lhsT_scale=xs[:, g, m, :],
-                    rhs=wc[:].bitcast(FP8X4),
-                    rhs_scale=ws[:],
-                    start=(g == 0),
-                    stop=(g == PASSES - 1),
-                )
+                acc[(n, m)] = psum.tile([P, wd], F32, name="acc", tag="acc%d" % ((MT * n + m) % ACC_BANKS))
+                for g in range(PASSES):
+                    wc, ws = codes[PASSES * n + g]
+                    nc.tensor.matmul_mx(
+                        out=acc[(n, m)][:],
+                        lhsT=xc[:, g, m, :].bitcast(FP8X4),
+                        lhsT_scale=xs[:, g, m, :],
+                        rhs=wc[:].bitcast(FP8X4),
+                        rhs_scale=ws[:],
+                        start=(g == 0),
+                        stop=(g == PASSES - 1),
+                    )
 
         def result_tile(n):
             tens, lc = divmod(TILES[n][0], TCOLS)
@@ -256,12 +274,15 @@ def tile_attention_pa_kernel(tc, x, f1, f2, f3, Wqkv_bytes, Wqkv_scale, out_0, o
             if k == TABLE_STEP:
                 tables()
             if 0 <= k - 1 < NCH:
-                interleave(k - 1)
+                interleave_s(k - 1)
+            if 0 <= k - 2 < NCH:
+                interleave_v(k - 2)
             pn, pstep = divmod(k - LAG, 3)
             if 0 <= pn < NT:
                 post(pn, 2 * pstep)
-            if 0 <= k - 2 < NCH:
-                quantize(k - 2)
-                matmuls(k - 2)
+            if 0 <= k - 3 < NCH:
+                quantize(k - 3)
+                if (k - 3) % PASSES == PASSES - 1:
+                    matmuls((k - 3) // PASSES)
             if 0 <= pn < NT:
                 post(pn, 2 * pstep + 1)

@@ -27,13 +27,11 @@ TILES = tuple((NB * i, NB) for i in range(8)) + ((4096, 256), (4352, 128), (4480
 NT = len(TILES)
 NCH = NT * PASSES
 ROPED = 6
-ACC_BANKS = 6
 
 FLOPS = 2 * TOK * DIM * COLS
 
-VCOLS = (400, 256, 176, 176, 176, 176, 176, 176, 256, 128, 128)
-PCOLS = (0, 256, 256, 256, 256, 256, 256, 256, 0, 0, 0)
-LAG = 6
+VCOLS = (400, 400, 272, 272, 272, 272, 272, 272, 256, 128, 128)
+LAG = 5
 TABLE_STEP = 2
 
 
@@ -79,8 +77,6 @@ def tile_attention_pa_kernel(tc, x, f1, f2, f3, Wqkv_bytes, Wqkv_scale, out_0, o
 
         ident = const.tile([P, P], F32, name="ident")
         make_identity(nc, ident[:])
-        identb = const.tile([P, P], BF16, name="identb")
-        make_identity(nc, identb[:])
 
         cos_t = const.tile([P, 2, TABW], F32, name="cos_t")
         ssw_t = const.tile([P, 2, TABW], F32, name="ssw_t")
@@ -114,7 +110,7 @@ def tile_attention_pa_kernel(tc, x, f1, f2, f3, Wqkv_bytes, Wqkv_scale, out_0, o
         xgs = {}
 
         def x_turn(mp, g):
-            xt = psum.tile([P, 2, 2, P], F32, name="xt", tag="acc%d" % (3 * mp + g))
+            xt = psum.tile([P, 2, 2, P], F32, name="xt", tag="bank%d" % (3 * mp + g))
             for mi in range(2):
                 words = x_sb[2 * mp + mi][:].bitcast(F32)
                 for u in range(2):
@@ -158,32 +154,23 @@ def tile_attention_pa_kernel(tc, x, f1, f2, f3, Wqkv_bytes, Wqkv_scale, out_0, o
                 )
             planes[c] = pl
 
-        def interleave_s(c):
+        def interleave(c):
             n = c // PASSES
             wd = TILES[n][1]
             vc = VCOLS[n]
-            pcn = PCOLS[n]
             pl = planes[c]
             il = stage.tile([P, wd, 4], BF16, name="il", tag="il", bufs=4, align_bytes=64)
+            if vc > 0:
+                nc.vector.tensor_copy(
+                    out=il[:, 0:vc, :].rearrange("p (c i) t -> p c t i", i=4),
+                    in_=pl[:, :, 0:vc].rearrange("p t (c i) -> p c t i", i=4),
+                )
+            if vc < wd:
+                nc.scalar.copy(
+                    out=il[:, vc:wd, :].rearrange("p (c i) t -> p c t i", i=4),
+                    in_=pl[:, :, vc:wd].rearrange("p t (c i) -> p c t i", i=4),
+                )
             inter[c] = il
-            if pcn > 0:
-                pb = psum.tile([P, 4 * pcn], BF16, name="pb", tag="pb%d" % (c % 2))
-                for c0 in range(0, pcn, P):
-                    w = min(P, pcn - c0)
-                    nc.tensor.matmul(
-                        out=pb[:, 4 * c0 : 4 * (c0 + w)],
-                        lhsT=identb[:],
-                        rhs=pl[:, :, vc + c0 : vc + c0 + w].rearrange("p t c -> p c t"),
-                        start=True,
-                        stop=True,
-                    )
-                nc.scalar.copy(out=il[:, vc : vc + pcn, :].rearrange("p c t -> p (c t)"), in_=pb[:])
-            if vc + pcn < wd:
-                nc.scalar.copy(out=il[:, vc + pcn : wd, :], in_=pl[:, :, vc + pcn : wd].rearrange("p t c -> p c t"))
-
-        def interleave_v(c):
-            vc = VCOLS[c // PASSES]
-            nc.vector.tensor_copy(out=inter[c][:, 0:vc, :], in_=planes[c][:, :, 0:vc].rearrange("p t c -> p c t"))
 
         def quantize(c):
             wd = TILES[c // PASSES][1]
@@ -194,21 +181,22 @@ def tile_attention_pa_kernel(tc, x, f1, f2, f3, Wqkv_bytes, Wqkv_scale, out_0, o
             )
             codes[c] = (wc, ws)
 
-        def matmuls(n):
+        def matmuls(c):
+            n, g = divmod(c, PASSES)
             wd = TILES[n][1]
+            wc, ws = codes[c]
             for m in range(MT):
-                acc[(n, m)] = psum.tile([P, wd], F32, name="acc", tag="acc%d" % ((MT * n + m) % ACC_BANKS))
-                for g in range(PASSES):
-                    wc, ws = codes[PASSES * n + g]
-                    nc.tensor.matmul_mx(
-                        out=acc[(n, m)][:],
-                        lhsT=xc[:, g, m, :].bitcast(FP8X4),
-                        lhsT_scale=xs[:, g, m, :],
-                        rhs=wc[:].bitcast(FP8X4),
-                        rhs_scale=ws[:],
-                        start=(g == 0),
-                        stop=(g == PASSES - 1),
-                    )
+                if g == 0:
+                    acc[(n, m)] = psum.tile([P, wd], F32, name="acc", tag="bank%d" % (4 * (n % 2) + m))
+                nc.tensor.matmul_mx(
+                    out=acc[(n, m)][:],
+                    lhsT=xc[:, g, m, :].bitcast(FP8X4),
+                    lhsT_scale=xs[:, g, m, :],
+                    rhs=wc[:].bitcast(FP8X4),
+                    rhs_scale=ws[:],
+                    start=(g == 0),
+                    stop=(g == PASSES - 1),
+                )
 
         def result_tile(n):
             tens, lc = divmod(TILES[n][0], TCOLS)
@@ -274,15 +262,12 @@ def tile_attention_pa_kernel(tc, x, f1, f2, f3, Wqkv_bytes, Wqkv_scale, out_0, o
             if k == TABLE_STEP:
                 tables()
             if 0 <= k - 1 < NCH:
-                interleave_s(k - 1)
-            if 0 <= k - 2 < NCH:
-                interleave_v(k - 2)
+                interleave(k - 1)
             pn, pstep = divmod(k - LAG, 3)
             if 0 <= pn < NT:
                 post(pn, 2 * pstep)
-            if 0 <= k - 3 < NCH:
-                quantize(k - 3)
-                if (k - 3) % PASSES == PASSES - 1:
-                    matmuls((k - 3) // PASSES)
+            if 0 <= k - 2 < NCH:
+                quantize(k - 2)
+                matmuls(k - 2)
             if 0 <= pn < NT:
                 post(pn, 2 * pstep + 1)

@@ -30,8 +30,10 @@ ROPED = 6
 
 FLOPS = 2 * TOK * DIM * COLS
 
-VCOLS = (400, 400, 272, 272, 272, 272, 272, 272, 256, 128, 128)
-LAG = 5
+VCOLS = (304, 304, 328, 328, 328, 328, 224, 512, 256, 128, 128)
+GM = 3
+S_EVAC = ((0,), (0, 2), (0, 2), (0, 2), (0, 2))
+V_WIDENS = 1
 TABLE_STEP = 2
 
 
@@ -65,21 +67,22 @@ def tile_attention_pa_kernel(tc, x, f1, f2, f3, Wqkv_bytes, Wqkv_scale, out_0, o
             nc.sync.dma_start(out=t[:], in_=wview[g][:, :, c0 : c0 + wd])
             wb.append(t)
 
-        load_w(0)
+        for c in range(V_WIDENS + 1):
+            load_w(c)
         for m in range(MT):
             t = const.tile([P, DIM], BF16, name="x%d" % m)
             nc.sync.dma_start(out=t[:], in_=xf[P * m : P * (m + 1), :])
             x_sb.append(t)
         for gi, f in enumerate((f1, f2, f3)):
             nc.sync.dma_start(out=fsb[:, :, 32 * gi : 32 * gi + 32], in_=f.rearrange("(h p) j -> p h j", p=P))
-        for c in range(1, NCH):
+        for c in range(V_WIDENS + 1, NCH):
             load_w(c)
 
         ident = const.tile([P, P], F32, name="ident")
         make_identity(nc, ident[:])
+        junk = const.tile([P, 8], F32, name="junk")
 
-        cos_t = const.tile([P, 2, TABW], F32, name="cos_t")
-        ssw_t = const.tile([P, 2, TABW], F32, name="ssw_t")
+        tab = const.tile([P, 2, 2, TABW], F32, name="tab")
 
         def tables():
             sh = const.tile([P, 2, DH], F32, name="sh")
@@ -93,17 +96,46 @@ def tile_attention_pa_kernel(tc, x, f1, f2, f3, Wqkv_bytes, Wqkv_scale, out_0, o
             nc.vector.tensor_tensor(out=sq[:], in0=sh[:], in1=sh[:], op=ALU.mult)
             reps = TABW // DH
             nc.vector.tensor_copy(
-                out=ssw_t[:].rearrange("p h (r d) -> p h r d", d=DH),
+                out=tab[:, :, 1, :].rearrange("p h (r d) -> p h r d", d=DH),
                 in_=sswb[:].unsqueeze(2).to_broadcast([P, 2, reps, DH]),
             )
             nc.vector.tensor_scalar(
-                out=cos_t[:].rearrange("p h (r d) -> p h r d", d=DH),
+                out=tab[:, :, 0, :].rearrange("p h (r d) -> p h r d", d=DH),
                 in0=sq[:].unsqueeze(2).to_broadcast([P, 2, reps, DH]),
                 scalar1=-2.0,
                 scalar2=1.0,
                 op0=ALU.mult,
                 op1=ALU.add,
             )
+
+        planes = {}
+        inter = {}
+        codes = {}
+        acc = {}
+        prod = {}
+        res = {}
+
+        def widen(c):
+            n, g = divmod(c, PASSES)
+            wd = TILES[n][1]
+            pl = stage.tile([P, 4, wd], BF16, name="pl", tag="pl", bufs=5)
+            for t in range(4):
+                if c < V_WIDENS:
+                    nc.vector.tensor_scalar(
+                        out=pl[:, t, :],
+                        in0=wb[c][:, t, :].bitcast(FP8),
+                        scalar1=wsc[:, g, t : t + 1],
+                        scalar2=None,
+                        op0=ALU.mult,
+                    )
+                else:
+                    nc.scalar.activation(
+                        out=pl[:, t, :], in_=wb[c][:, t, :].bitcast(FP8), func=ACT.Copy, scale=wsc[:, g, t : t + 1]
+                    )
+            planes[c] = pl
+
+        for c in range(V_WIDENS):
+            widen(c)
 
         xc = const.tile([P, PASSES, MT, P], U32, name="xc", align_bytes=64)
         xs = const.tile([P, PASSES, MT, P], U8, name="xs", align_bytes=64)
@@ -115,7 +147,7 @@ def tile_attention_pa_kernel(tc, x, f1, f2, f3, Wqkv_bytes, Wqkv_scale, out_0, o
                 words = x_sb[2 * mp + mi][:].bitcast(F32)
                 for u in range(2):
                     nc.tensor.transpose(xt[:, mi, u, :], words[:, 256 * g + u : 256 * (g + 1) : 2], ident[:])
-            xg = stage.tile([P, 2 * P * 4], BF16, name="xg", tag="xg", bufs=3, align_bytes=64)
+            xg = stage.tile([P, 2 * P * 4], BF16, name="xg", tag="xg", bufs=2, align_bytes=64)
             nc.vector.tensor_copy(
                 out=xg[:].bitcast(F32).rearrange("p (m r u) -> p m r u", m=2, u=2),
                 in_=xt[:].rearrange("p m u r -> p m r u"),
@@ -136,30 +168,12 @@ def tile_attention_pa_kernel(tc, x, f1, f2, f3, Wqkv_bytes, Wqkv_scale, out_0, o
                 x_quant(*xorder[i - 1])
         x_quant(*xorder[-1])
 
-        planes = {}
-        inter = {}
-        codes = {}
-        acc = {}
-        prod_c = {}
-        prod_s = {}
-        res = {}
-
-        def widen(c):
-            n, g = divmod(c, PASSES)
-            wd = TILES[n][1]
-            pl = stage.tile([P, 4, wd], BF16, name="pl", tag="pl", bufs=4)
-            for t in range(4):
-                nc.scalar.activation(
-                    out=pl[:, t, :], in_=wb[c][:, t, :].bitcast(FP8), func=ACT.Copy, scale=wsc[:, g, t : t + 1]
-                )
-            planes[c] = pl
-
         def interleave(c):
             n = c // PASSES
             wd = TILES[n][1]
             vc = VCOLS[n]
             pl = planes[c]
-            il = stage.tile([P, wd, 4], BF16, name="il", tag="il", bufs=4, align_bytes=64)
+            il = stage.tile([P, wd, 4], BF16, name="il", tag="il", bufs=5, align_bytes=64)
             if vc > 0:
                 nc.vector.tensor_copy(
                     out=il[:, 0:vc, :].rearrange("p (c i) t -> p c t i", i=4),
@@ -174,8 +188,8 @@ def tile_attention_pa_kernel(tc, x, f1, f2, f3, Wqkv_bytes, Wqkv_scale, out_0, o
 
         def quantize(c):
             wd = TILES[c // PASSES][1]
-            wc = stage.tile([P, wd], U32, name="wc", tag="wc", bufs=6, align_bytes=64)
-            ws = stage.tile([P, wd], U8, name="ws", tag="ws", bufs=6, align_bytes=64)
+            wc = stage.tile([P, wd], U32, name="wc", tag="wc", bufs=4, align_bytes=64)
+            ws = stage.tile([P, wd], U8, name="ws", tag="ws", bufs=4, align_bytes=64)
             nc.vector.quantize_mx(
                 out=wc[:].bitcast(FP8X4), scales=ws[:], in_=inter[c][:].rearrange("p c t -> p (c t)")
             )
@@ -204,25 +218,24 @@ def tile_attention_pa_kernel(tc, x, f1, f2, f3, Wqkv_bytes, Wqkv_scale, out_0, o
                 res[tens] = stage.tile([P, MT, TCOLS], F32, name="res", tag="res", bufs=2)
             return res[tens], lc
 
-        def mults(n, m):
+        def products(n, m):
             if m == 0:
-                prod_c[n] = stage.tile([P, MT, NB], F32, name="pc", tag="pc", bufs=2)
-                prod_s[n] = stage.tile([P, MT, NB], F32, name="ps", tag="ps", bufs=2)
+                prod[n] = stage.tile([P, MT, 2, NB], F32, name="prod", tag="prod", bufs=2)
             off = TILES[n][0] % DH
-            th = m % 2
             nc.vector.tensor_tensor(
-                out=prod_c[n][:, m, :], in0=acc[(n, m)][:], in1=cos_t[:, th, off : off + NB], op=ALU.mult
-            )
-            nc.vector.tensor_tensor(
-                out=prod_s[n][:, m, :], in0=acc[(n, m)][:], in1=ssw_t[:, th, off : off + NB], op=ALU.mult
+                out=prod[n][:, m, :, :],
+                in0=acc[(n, m)][:].unsqueeze(1).to_broadcast([P, 2, NB]),
+                in1=tab[:, m % 2, :, off : off + NB],
+                op=ALU.mult,
             )
 
-        def add_half(n, e):
+        def sums(eng, n, m0, m1):
             r, lc = result_tile(n)
-            rv = r[:, :, lc : lc + NB].rearrange("p m (g e i) -> p m g e i", e=2, i=16)
-            cv = prod_c[n][:].rearrange("p m (g e i) -> p m g e i", e=2, i=16)
-            sv2 = prod_s[n][:].rearrange("p m (g e i) -> p m g e i", e=2, i=16)
-            nc.vector.tensor_tensor(out=rv[:, :, :, e, :], in0=cv[:, :, :, e, :], in1=sv2[:, :, :, 1 - e, :], op=ALU.add)
+            rv = r[:, m0:m1, lc : lc + NB].rearrange("p m (g e i) -> p m g e i", e=2, i=16)
+            cv = prod[n][:, m0:m1, 0, :].rearrange("p m (g e i) -> p m g e i", e=2, i=16)
+            sv = prod[n][:, m0:m1, 1, :].rearrange("p m (g e i) -> p m g e i", e=2, i=16)
+            for e in range(2):
+                eng.tensor_tensor(out=rv[:, :, :, e, :], in0=cv[:, :, :, e, :], in1=sv[:, :, :, 1 - e, :], op=ALU.add)
 
         def store(n, m):
             r, lc = result_tile(n)
@@ -238,36 +251,41 @@ def tile_attention_pa_kernel(tc, x, f1, f2, f3, Wqkv_bytes, Wqkv_scale, out_0, o
         def evac(n, m):
             r, lc = result_tile(n)
             wd = TILES[n][1]
-            if m % 2 == 0:
+            if m in S_EVAC[n - ROPED]:
                 nc.scalar.copy(out=r[:, m, lc : lc + wd], in_=acc[(n, m)][:])
             else:
                 nc.vector.tensor_copy(out=r[:, m, lc : lc + wd], in_=acc[(n, m)][:])
             store(n, m)
 
-        def post(n, part):
+        def block(n):
+            if 1 <= n < ROPED and GM > 0:
+                sums(nc.vector, n - 1, GM, MT)
+                r, lc = result_tile(n - 1)
+                nc.gpsimd.tensor_copy(out=junk[:, 0:1], in_=r[:, MT - 1, lc + 16 : lc + 17])
+                sums(nc.gpsimd, n - 1, 0, GM)
             if n < ROPED:
-                if part < 4:
-                    mults(n, part)
-                else:
-                    add_half(n, part - 4)
-                    if part == 5:
-                        for m in range(MT):
-                            store(n, m)
-            elif part < 4:
-                evac(n, part)
+                for m in range(MT):
+                    products(n, m)
+                if n >= 1 and GM > 0:
+                    for m in range(MT):
+                        store(n - 1, m)
+                if n == ROPED - 1 or GM == 0:
+                    sums(nc.vector, n, 0, MT)
+                    for m in range(MT):
+                        store(n, m)
+            else:
+                for m in range(MT):
+                    evac(n, m)
 
-        for k in range(NCH + LAG + 3):
-            if k < NCH:
+        for k in range(NCH + 4):
+            if V_WIDENS <= k < NCH:
                 widen(k)
             if k == TABLE_STEP:
                 tables()
             if 0 <= k - 1 < NCH:
                 interleave(k - 1)
-            pn, pstep = divmod(k - LAG, 3)
-            if 0 <= pn < NT:
-                post(pn, 2 * pstep)
             if 0 <= k - 2 < NCH:
                 quantize(k - 2)
                 matmuls(k - 2)
-            if 0 <= pn < NT:
-                post(pn, 2 * pstep + 1)
+            if (k - 1) % PASSES == PASSES - 1 and k > PASSES:
+                block((k - 1) // PASSES - 1)

@@ -30,10 +30,10 @@ ROPED = 6
 
 FLOPS = 2 * TOK * DIM * COLS
 
-VCOLS = (304, 304, 328, 328, 328, 328, 224, 512, 256, 128, 128)
+VCOLS = (304, 304, 352, 352, 352, 352, 248, 512, 256, 128, 128)
 GM = 3
-S_EVAC = ((0,), (0, 2), (0, 2), (0, 2), (0, 2))
-V_WIDENS = 1
+S_EVAC = ((0, 1, 2, 3), (0, 1, 2, 3), (0, 2), (0, 2), (0, 2))
+V_WIDENS = 2
 TABLE_STEP = 2
 
 

@@ -30,11 +30,11 @@ ROPED = 6
 
 FLOPS = 2 * TOK * DIM * COLS
 
-VCOLS = (304, 304, 352, 352, 352, 352, 248, 512, 256, 128, 128)
+VCOLS = (304, 304, 352, 352, 352, 352, 248, 384, 256, 128, 128)
 GM = 3
 S_EVAC = ((0, 1, 2, 3), (0, 1, 2, 3), (0, 2), (0, 2), (0, 2))
 V_WIDENS = 2
-TABLE_STEP = 2
+EVAC_LAG = 2
 
 
 def tile_attention_pa_kernel(tc, x, f1, f2, f3, Wqkv_bytes, Wqkv_scale, out_0, out_1, out_2):
@@ -56,7 +56,6 @@ def tile_attention_pa_kernel(tc, x, f1, f2, f3, Wqkv_bytes, Wqkv_scale, out_0, o
         nc.scalar.activation(out=warm[:, 1:2], in_=warm[:, 0:1], func=ACT.Sin)
 
         wview = Wqkv_bytes.rearrange("(g p t) c -> g p t c", p=P, t=4)
-        xf = x.flatten_outer_dims()
         wb = []
         x_sb = []
 
@@ -67,15 +66,20 @@ def tile_attention_pa_kernel(tc, x, f1, f2, f3, Wqkv_bytes, Wqkv_scale, out_0, o
             nc.sync.dma_start(out=t[:], in_=wview[g][:, :, c0 : c0 + wd])
             wb.append(t)
 
-        for c in range(V_WIDENS + 1):
-            load_w(c)
-        for m in range(MT):
-            t = const.tile([P, DIM], BF16, name="x%d" % m)
-            nc.sync.dma_start(out=t[:], in_=xf[P * m : P * (m + 1), :])
+        def load_x(b):
+            t = const.tile([P, 2, DIM], BF16, name="x%d" % b)
+            nc.sync.dma_start(out=t[:], in_=x[b].rearrange("(p e) k -> p e k", e=2))
             x_sb.append(t)
+
+        for c in range(2):
+            load_w(c)
         for gi, f in enumerate((f1, f2, f3)):
-            nc.sync.dma_start(out=fsb[:, :, 32 * gi : 32 * gi + 32], in_=f.rearrange("(h p) j -> p h j", p=P))
-        for c in range(V_WIDENS + 1, NCH):
+            nc.sync.dma_start(out=fsb[:, :, 32 * gi : 32 * gi + 32], in_=f.rearrange("(p e) j -> p e j", e=2))
+        load_w(2)
+        load_x(0)
+        load_w(3)
+        load_x(1)
+        for c in range(4, NCH):
             load_w(c)
 
         ident = const.tile([P, P], F32, name="ident")
@@ -84,14 +88,17 @@ def tile_attention_pa_kernel(tc, x, f1, f2, f3, Wqkv_bytes, Wqkv_scale, out_0, o
 
         tab = const.tile([P, 2, 2, TABW], F32, name="tab")
 
-        def tables():
-            sh = const.tile([P, 2, DH], F32, name="sh")
+        sh = const.tile([P, 2, DH], F32, name="sh")
+        sswb = const.tile([P, 2, DH], F32, name="sswb")
+
+        def tables_s():
             nc.scalar.activation(out=sh[:], in_=fsb[:], func=ACT.Sin, scale=0.5)
-            sswb = const.tile([P, 2, DH], F32, name="sswb")
             fv = fsb[:].rearrange("p h (g e i) -> p (h g) e i", e=2, i=16)
             sv = sswb[:].rearrange("p h (g e i) -> p (h g) e i", e=2, i=16)
             nc.scalar.activation(out=sv[:, :, 0, :], in_=fv[:, :, 1, :], func=ACT.Sin)
             nc.scalar.activation(out=sv[:, :, 1, :], in_=fv[:, :, 0, :], func=ACT.Sin, scale=-1.0)
+
+        def tables_v():
             sq = const.tile([P, 2, DH], F32, name="sq")
             nc.vector.tensor_tensor(out=sq[:], in0=sh[:], in1=sh[:], op=ALU.mult)
             reps = TABW // DH
@@ -134,8 +141,10 @@ def tile_attention_pa_kernel(tc, x, f1, f2, f3, Wqkv_bytes, Wqkv_scale, out_0, o
                     )
             planes[c] = pl
 
+        tables_s()
         for c in range(V_WIDENS):
             widen(c)
+        tables_v()
 
         xc = const.tile([P, PASSES, MT, P], U32, name="xc", align_bytes=64)
         xs = const.tile([P, PASSES, MT, P], U8, name="xs", align_bytes=64)
@@ -144,7 +153,7 @@ def tile_attention_pa_kernel(tc, x, f1, f2, f3, Wqkv_bytes, Wqkv_scale, out_0, o
         def x_turn(mp, g):
             xt = psum.tile([P, 2, 2, P], F32, name="xt", tag="bank%d" % (3 * mp + g))
             for mi in range(2):
-                words = x_sb[2 * mp + mi][:].bitcast(F32)
+                words = x_sb[mp][:, mi, :].bitcast(F32)
                 for u in range(2):
                     nc.tensor.transpose(xt[:, mi, u, :], words[:, 256 * g + u : 256 * (g + 1) : 2], ident[:])
             xg = stage.tile([P, 2 * P * 4], BF16, name="xg", tag="xg", bufs=2, align_bytes=64)
@@ -161,17 +170,11 @@ def tile_attention_pa_kernel(tc, x, f1, f2, f3, Wqkv_bytes, Wqkv_scale, out_0, o
                 in_=xgs[(mp, g)][:],
             )
 
-        xorder = [(mp, g) for mp in range(2) for g in range(PASSES)]
-        for i, (mp, g) in enumerate(xorder):
-            x_turn(mp, g)
-            if i >= 1:
-                x_quant(*xorder[i - 1])
-        x_quant(*xorder[-1])
 
         def interleave(c):
             n = c // PASSES
             wd = TILES[n][1]
-            vc = VCOLS[n]
+            vc = wd if c < V_WIDENS else VCOLS[n]
             pl = planes[c]
             il = stage.tile([P, wd, 4], BF16, name="il", tag="il", bufs=5, align_bytes=64)
             if vc > 0:
@@ -242,20 +245,41 @@ def tile_attention_pa_kernel(tc, x, f1, f2, f3, Wqkv_bytes, Wqkv_scale, out_0, o
             tens = TILES[n][0] // TCOLS
             h0 = lc // DH
             h1 = (lc + TILES[n][1]) // DH
-            b, th = divmod(m, 2)
+            b, e = divmod(m, 2)
             nc.sync.dma_start(
-                out=outs[tens][b, h0:h1, P * th : P * (th + 1), :].rearrange("h n d -> n h d"),
+                out=outs[tens][b, h0:h1, :, :].rearrange("h (p e) d -> e p h d", e=2)[e],
                 in_=r[:, m, DH * h0 : DH * h1].rearrange("p (h d) -> p h d", d=DH),
             )
 
         def evac(n, m):
-            r, lc = result_tile(n)
+            if "v" not in res:
+                res["v"] = stage.tile([P, 2, HEADS, 2, DH], F32, name="res", tag="res", bufs=2)
+            rv = res["v"]
+            lc = TILES[n][0] % TCOLS
             wd = TILES[n][1]
-            if m in S_EVAC[n - ROPED]:
-                nc.scalar.copy(out=r[:, m, lc : lc + wd], in_=acc[(n, m)][:])
-            else:
-                nc.vector.tensor_copy(out=r[:, m, lc : lc + wd], in_=acc[(n, m)][:])
-            store(n, m)
+            b, e = divmod(m, 2)
+            eng_copy = nc.scalar.copy if m in S_EVAC[n - ROPED] else nc.vector.tensor_copy
+            pos = lc
+            while pos < lc + wd:
+                h, d0 = divmod(pos, DH)
+                if d0 == 0 and lc + wd - pos >= DH:
+                    nh = (lc + wd - pos) // DH
+                    eng_copy(
+                        out=rv[:, b, h : h + nh, e, :],
+                        in_=acc[(n, m)][:, pos - lc : pos - lc + DH * nh].rearrange("p (h d) -> p h d", d=DH),
+                    )
+                    pos += DH * nh
+                else:
+                    ln = min(DH - d0, lc + wd - pos)
+                    eng_copy(out=rv[:, b, h, e, d0 : d0 + ln], in_=acc[(n, m)][:, pos - lc : pos - lc + ln])
+                    pos += ln
+            if e == 1:
+                h0 = lc // DH
+                h1 = (lc + wd) // DH
+                nc.sync.dma_start(
+                    out=outs[2][b, h0:h1, :, :].rearrange("h (p e) d -> p h (e d)", e=2),
+                    in_=rv[:, b, h0:h1, :, :].rearrange("p h e d -> p h (e d)"),
+                )
 
         def block(n):
             if 1 <= n < ROPED and GM > 0:
@@ -273,19 +297,30 @@ def tile_attention_pa_kernel(tc, x, f1, f2, f3, Wqkv_bytes, Wqkv_scale, out_0, o
                     sums(nc.vector, n, 0, MT)
                     for m in range(MT):
                         store(n, m)
-            else:
-                for m in range(MT):
-                    evac(n, m)
+
+        for c in range(V_WIDENS):
+            interleave(c)
+        for c in range(V_WIDENS):
+            quantize(c)
+        xorder = [(mp, g) for mp in range(2) for g in range(PASSES)]
+        for i, (mp, g) in enumerate(xorder):
+            x_turn(mp, g)
+            if i >= 1:
+                x_quant(*xorder[i - 1])
+        x_quant(*xorder[-1])
 
         for k in range(NCH + 4):
             if V_WIDENS <= k < NCH:
                 widen(k)
-            if k == TABLE_STEP:
-                tables()
-            if 0 <= k - 1 < NCH:
+            if V_WIDENS <= k - 1 < NCH:
                 interleave(k - 1)
             if 0 <= k - 2 < NCH:
-                quantize(k - 2)
+                if k - 2 >= V_WIDENS:
+                    quantize(k - 2)
                 matmuls(k - 2)
             if (k - 1) % PASSES == PASSES - 1 and k > PASSES:
                 block((k - 1) // PASSES - 1)
+            for n in range(ROPED, NT):
+                if k == min(PASSES * n + 6 + EVAC_LAG, NCH + 3 - (NT - 1 - n)):
+                    for m in range(MT):
+                        evac(n, m)

@@ -179,13 +179,13 @@ def tile_attention_pa_kernel(tc, x, f1, f2, f3, Wqkv_bytes, Wqkv_scale, out_0, o
             il = stage.tile([P, wd, 4], BF16, name="il", tag="il", bufs=5, align_bytes=64)
             if vc > 0:
                 nc.vector.tensor_copy(
-                    out=il[:, 0:vc, :].rearrange("p (c i) t -> p c t i", i=4),
-                    in_=pl[:, :, 0:vc].rearrange("p t (c i) -> p c t i", i=4),
+                    out=il[:, 0:vc, :].rearrange("p (c i) t -> p c t i", i=8),
+                    in_=pl[:, :, 0:vc].rearrange("p t (c i) -> p c t i", i=8),
                 )
             if vc < wd:
                 nc.scalar.copy(
-                    out=il[:, vc:wd, :].rearrange("p (c i) t -> p c t i", i=4),
-                    in_=pl[:, :, vc:wd].rearrange("p t (c i) -> p c t i", i=4),
+                    out=il[:, vc:wd, :].rearrange("p (c i) t -> p c t i", i=8),
+                    in_=pl[:, :, vc:wd].rearrange("p t (c i) -> p c t i", i=8),
                 )
             inter[c] = il
 

@@ -32,7 +32,7 @@ FLOPS = 2 * TOK * DIM * COLS
 
 VCOLS = (304, 304, 352, 352, 352, 352, 248, 384, 256, 128, 128)
 GM = 3
-S_EVAC = ((0, 1, 2, 3), (0, 1, 2, 3), (0, 2), (0, 2), (0, 2))
+S_EVAC = ((0, 1, 2, 3), (0, 1, 2, 3), (0, 1, 2, 3), (0, 1, 2, 3), (0, 2))
 V_WIDENS = 2
 EVAC_LAG = 2
 
@@ -63,7 +63,11 @@ def tile_attention_pa_kernel(tc, x, f1, f2, f3, Wqkv_bytes, Wqkv_scale, out_0, o
             n, g = divmod(c, PASSES)
             c0, wd = TILES[n]
             t = wbp.tile([P, 4, wd], U8, name="wb%d" % c)
-            nc.sync.dma_start(out=t[:], in_=wview[g][:, :, c0 : c0 + wd])
+            if c == 0:
+                for j in range(4):
+                    nc.sync.dma_start(out=t[:, j, :], in_=wview[g][:, j, c0 : c0 + wd])
+            else:
+                nc.sync.dma_start(out=t[:], in_=wview[g][:, :, c0 : c0 + wd])
             wb.append(t)
 
         def load_x(b):
@@ -127,7 +131,7 @@ def tile_attention_pa_kernel(tc, x, f1, f2, f3, Wqkv_bytes, Wqkv_scale, out_0, o
             wd = TILES[n][1]
             pl = stage.tile([P, 4, wd], BF16, name="pl", tag="pl", bufs=5)
             for t in range(4):
-                if c < V_WIDENS:
+                if c < V_WIDENS and t < 2:
                     nc.vector.tensor_scalar(
                         out=pl[:, t, :],
                         in0=wb[c][:, t, :].bitcast(FP8),
@@ -141,10 +145,9 @@ def tile_attention_pa_kernel(tc, x, f1, f2, f3, Wqkv_bytes, Wqkv_scale, out_0, o
                     )
             planes[c] = pl
 
-        tables_s()
         for c in range(V_WIDENS):
             widen(c)
-        tables_v()
+        tables_s()
 
         xc = const.tile([P, PASSES, MT, P], U32, name="xc", align_bytes=64)
         xs = const.tile([P, PASSES, MT, P], U8, name="xs", align_bytes=64)
@@ -302,6 +305,7 @@ def tile_attention_pa_kernel(tc, x, f1, f2, f3, Wqkv_bytes, Wqkv_scale, out_0, o
             interleave(c)
         for c in range(V_WIDENS):
             quantize(c)
+        tables_v()
         xorder = [(mp, g) for mp in range(2) for g in range(PASSES)]
         for i, (mp, g) in enumerate(xorder):
             x_turn(mp, g)

@@ -30,7 +30,7 @@ ROPED = 6
 
 FLOPS = 2 * TOK * DIM * COLS
 
-VCOLS = (304, 304, 352, 352, 352, 352, 248, 384, 256, 128, 128)
+VCOLS = (320, 320, 368, 368, 368, 368, 248, 384, 256, 128, 128)
 GM = 3
 S_EVAC = ((0, 1, 2, 3), (0, 1, 2, 3), (0, 1, 2, 3), (0, 1, 2, 3), (0, 2))
 V_WIDENS = 2
@@ -106,15 +106,19 @@ def tile_attention_pa_kernel(tc, x, f1, f2, f3, Wqkv_bytes, Wqkv_scale, out_0, o
             sq = const.tile([P, 2, DH], F32, name="sq")
             nc.vector.tensor_tensor(out=sq[:], in0=sh[:], in1=sh[:], op=ALU.mult)
             reps = TABW // DH
-            nc.vector.tensor_copy(
-                out=tab[:, :, 1, :].rearrange("p h (r d) -> p h r d", d=DH),
-                in_=sswb[:].unsqueeze(2).to_broadcast([P, 2, reps, DH]),
-            )
-            nc.vector.tensor_scalar(
+            nc.gpsimd.tensor_scalar(
                 out=tab[:, :, 0, :].rearrange("p h (r d) -> p h r d", d=DH),
                 in0=sq[:].unsqueeze(2).to_broadcast([P, 2, reps, DH]),
                 scalar1=-2.0,
                 scalar2=1.0,
+                op0=ALU.mult,
+                op1=ALU.add,
+            )
+            nc.gpsimd.tensor_scalar(
+                out=tab[:, :, 1, :].rearrange("p h (r d) -> p h r d", d=DH),
+                in0=sswb[:].unsqueeze(2).to_broadcast([P, 2, reps, DH]),
+                scalar1=1.0,
+                scalar2=0.0,
                 op0=ALU.mult,
                 op1=ALU.add,
             )
@@ -159,7 +163,7 @@ def tile_attention_pa_kernel(tc, x, f1, f2, f3, Wqkv_bytes, Wqkv_scale, out_0, o
                 words = x_sb[mp][:, mi, :].bitcast(F32)
                 for u in range(2):
                     nc.tensor.transpose(xt[:, mi, u, :], words[:, 256 * g + u : 256 * (g + 1) : 2], ident[:])
-            xg = stage.tile([P, 2 * P * 4], BF16, name="xg", tag="xg", bufs=2, align_bytes=64)
+            xg = stage.tile([P, 2 * P * 4], BF16, name="xg", tag="xg", bufs=6, align_bytes=64)
             nc.vector.tensor_copy(
                 out=xg[:].bitcast(F32).rearrange("p (m r u) -> p m r u", m=2, u=2),
                 in_=xt[:].rearrange("p m u r -> p m r u"),
@@ -307,11 +311,10 @@ def tile_attention_pa_kernel(tc, x, f1, f2, f3, Wqkv_bytes, Wqkv_scale, out_0, o
             quantize(c)
         tables_v()
         xorder = [(mp, g) for mp in range(2) for g in range(PASSES)]
-        for i, (mp, g) in enumerate(xorder):
+        for mp, g in xorder:
             x_turn(mp, g)
-            if i >= 1:
-                x_quant(*xorder[i - 1])
-        x_quant(*xorder[-1])
+        for mp, g in xorder:
+            x_quant(mp, g)
 
         for k in range(NCH + 4):
             if V_WIDENS <= k < NCH:

@@ -35,6 +35,7 @@ GM = 3
 S_EVAC = ((0, 1, 2, 3), (0, 1, 2, 3), (0, 1, 2, 3), (0, 1, 2, 3), (0, 2))
 V_WIDENS = 2
 EVAC_LAG = 2
+V_TAIL = (32,)
 
 
 def tile_attention_pa_kernel(tc, x, f1, f2, f3, Wqkv_bytes, Wqkv_scale, out_0, out_1, out_2):
@@ -63,7 +64,7 @@ def tile_attention_pa_kernel(tc, x, f1, f2, f3, Wqkv_bytes, Wqkv_scale, out_0, o
             n, g = divmod(c, PASSES)
             c0, wd = TILES[n]
             t = wbp.tile([P, 4, wd], U8, name="wb%d" % c)
-            if c == 0:
+            if c < 2:
                 for j in range(4):
                     nc.sync.dma_start(out=t[:, j, :], in_=wview[g][:, j, c0 : c0 + wd])
             else:
@@ -135,7 +136,7 @@ def tile_attention_pa_kernel(tc, x, f1, f2, f3, Wqkv_bytes, Wqkv_scale, out_0, o
             wd = TILES[n][1]
             pl = stage.tile([P, 4, wd], BF16, name="pl", tag="pl", bufs=5)
             for t in range(4):
-                if c < V_WIDENS and t < 2:
+                if (c < V_WIDENS and t < 2) or c in V_TAIL:
                     nc.vector.tensor_scalar(
                         out=pl[:, t, :],
                         in0=wb[c][:, t, :].bitcast(FP8),

@@ -35,6 +35,8 @@ GM = 3
 S_EVAC = ((0, 1, 2, 3), (0, 1, 2, 3), (0, 1, 2, 3), (0, 1, 2, 3), (0, 2))
 V_WIDENS = 2
 EVAC_LAG = 2
+G_CHUNK = 6
+G_COLS = 512
 V_TAIL = (32,)
 
 
@@ -90,6 +92,7 @@ def tile_attention_pa_kernel(tc, x, f1, f2, f3, Wqkv_bytes, Wqkv_scale, out_0, o
         ident = const.tile([P, P], F32, name="ident")
         make_identity(nc, ident[:])
         junk = const.tile([P, 8], F32, name="junk")
+        junku = const.tile([P, 8], U32, name="junku")
 
         tab = const.tile([P, 2, 2, TABW], F32, name="tab")
 
@@ -179,12 +182,20 @@ def tile_attention_pa_kernel(tc, x, f1, f2, f3, Wqkv_bytes, Wqkv_scale, out_0, o
             )
 
 
+        def il_tile(c):
+            if c not in inter:
+                inter[c] = stage.tile([P, TILES[c // PASSES][1], 4], BF16, name="il", tag="il", bufs=5, align_bytes=64)
+            return inter[c]
+
         def interleave(c):
             n = c // PASSES
             wd = TILES[n][1]
             vc = wd if c < V_WIDENS else VCOLS[n]
             pl = planes[c]
-            il = stage.tile([P, wd, 4], BF16, name="il", tag="il", bufs=5, align_bytes=64)
+            il = il_tile(c)
+            if c == G_CHUNK and G_COLS > 0:
+                wd = wd - G_COLS
+                vc = min(vc, wd)
             if vc > 0:
                 nc.vector.tensor_copy(
                     out=il[:, 0:vc, :].rearrange("p (c i) t -> p c t i", i=8),
@@ -196,6 +207,19 @@ def tile_attention_pa_kernel(tc, x, f1, f2, f3, Wqkv_bytes, Wqkv_scale, out_0, o
                     in_=pl[:, :, vc:wd].rearrange("p t (c i) -> p c t i", i=8),
                 )
             inter[c] = il
+
+        def g_interleave():
+            il = il_tile(G_CHUNK)
+            pl = planes[G_CHUNK]
+            nc.gpsimd.tensor_copy(out=junku[:, 0:1], in_=codes[4][0][:, 0:1])
+            nc.gpsimd.tensor_scalar(
+                out=il[:, NB - G_COLS : NB, :].rearrange("p (c i) t -> p c t i", i=8),
+                in0=pl[:, :, NB - G_COLS : NB].rearrange("p t (c i) -> p c t i", i=8),
+                scalar1=1.0,
+                scalar2=0.0,
+                op0=ALU.mult,
+                op1=ALU.add,
+            )
 
         def quantize(c):
             wd = TILES[c // PASSES][1]
@@ -295,6 +319,8 @@ def tile_attention_pa_kernel(tc, x, f1, f2, f3, Wqkv_bytes, Wqkv_scale, out_0, o
                 r, lc = result_tile(n - 1)
                 nc.gpsimd.tensor_copy(out=junk[:, 0:1], in_=r[:, MT - 1, lc + 16 : lc + 17])
                 sums(nc.gpsimd, n - 1, 0, GM)
+            if n == 0 and G_COLS > 0:
+                g_interleave()
             if n < ROPED:
                 for m in range(MT):
                     products(n, m)

from contextlib import ExitStack

import concourse.mybir as mybir
from concourse.masks import make_identity

F32 = mybir.dt.float32
BF16 = mybir.dt.bfloat16
U32 = mybir.dt.uint32
U8 = mybir.dt.uint8
FP8 = mybir.dt.float8_e4m3fn
FP8X4 = mybir.dt.float8_e4m3fn_x4
ACT = mybir.ActivationFunctionType
ALU = mybir.AluOpType

P = 128
TOK = 512
DIM = 1536
COLS = 4608
HEADS = 16
DH = 96
TCOLS = HEADS * DH
NB = 512
PASSES = 3
MT = TOK // P
TABW = 576
TILES = tuple((NB * i, NB) for i in range(8)) + ((4096, 256), (4352, 128), (4480, 128))
NT = len(TILES)
NCH = NT * PASSES
ROPED = 6

FLOPS = 2 * TOK * DIM * COLS

VCOLS = (320, 320, 368, 368, 368, 368, 248, 384, 256, 128, 128)
GM = 3
S_EVAC = ((0, 1, 2, 3), (0, 1, 2, 3), (0, 1, 2, 3), (0, 1, 2, 3), (0, 2))
V_WIDENS = 2
EVAC_LAG = 2
G_CHUNK = 6
G_COLS = 512
V_TAIL = (32,)


def tile_attention_pa_kernel(tc, x, f1, f2, f3, Wqkv_bytes, Wqkv_scale, out_0, out_1, out_2):
    nc = tc.nc
    outs = (out_0, out_1, out_2)

    with ExitStack() as ctx:
        const = ctx.enter_context(tc.tile_pool(name="const", bufs=1))
        wbp = ctx.enter_context(tc.tile_pool(name="wbytes", bufs=1))
        stage = ctx.enter_context(tc.tile_pool(name="stage", bufs=4))
        psum = ctx.enter_context(tc.psum_pool(name="psum", bufs=1))
        ctx.enter_context(tc.manual_schedule())

        wsc = const.tile([P, PASSES, 4], F32, name="wsc")
        nc.scalar.dma_start(out=wsc[:], in_=Wqkv_scale.rearrange("(g p t) o -> p g (t o)", p=P, t=4))
        fsb = const.tile([P, 2, DH], BF16, name="fsb")
        warm = const.tile([P, 2], F32, name="warm")
        nc.vector.memset(warm[:], 0.0)
        nc.scalar.activation(out=warm[:, 1:2], in_=warm[:, 0:1], func=ACT.Sin)

        wview = Wqkv_bytes.rearrange("(g p t) c -> g p t c", p=P, t=4)
        wb = []
        x_sb = []

        def load_w(c):
            n, g = divmod(c, PASSES)
            c0, wd = TILES[n]
            t = wbp.tile([P, 4, wd], U8, name="wb%d" % c)
            if c < 2:
                for j in range(4):
                    nc.sync.dma_start(out=t[:, j, :], in_=wview[g][:, j, c0 : c0 + wd])
            else:
                nc.sync.dma_start(out=t[:], in_=wview[g][:, :, c0 : c0 + wd])
            wb.append(t)

        def load_x(b):
            t = const.tile([P, 2, DIM], BF16, name="x%d" % b)
            nc.sync.dma_start(out=t[:], in_=x[b].rearrange("(p e) k -> p e k", e=2))
            x_sb.append(t)

        for c in range(2):
            load_w(c)
        for gi, f in enumerate((f1, f2, f3)):
            nc.sync.dma_start(out=fsb[:, :, 32 * gi : 32 * gi + 32], in_=f.rearrange("(p e) j -> p e j", e=2))
        load_w(2)
        load_x(0)
        load_w(3)
        load_x(1)
        for c in range(4, NCH):
            load_w(c)

        ident = const.tile([P, P], F32, name="ident")
        make_identity(nc, ident[:])
        junk = const.tile([P, 8], F32, name="junk")
        junku = const.tile([P, 8], U32, name="junku")

        tab = const.tile([P, 2, 2, TABW], F32, name="tab")

        sh = const.tile([P, 2, DH], F32, name="sh")
        sswb = const.tile([P, 2, DH], F32, name="sswb")

        def tables_s():
            nc.scalar.activation(out=sh[:], in_=fsb[:], func=ACT.Sin, scale=0.5)
            fv = fsb[:].rearrange("p h (g e i) -> p (h g) e i", e=2, i=16)
            sv = sswb[:].rearrange("p h (g e i) -> p (h g) e i", e=2, i=16)
            nc.scalar.activation(out=sv[:, :, 0, :], in_=fv[:, :, 1, :], func=ACT.Sin)
            nc.scalar.activation(out=sv[:, :, 1, :], in_=fv[:, :, 0, :], func=ACT.Sin, scale=-1.0)

        def tables_v():
            sq = const.tile([P, 2, DH], F32, name="sq")
            nc.vector.tensor_tensor(out=sq[:], in0=sh[:], in1=sh[:], op=ALU.mult)
            reps = TABW // DH
            nc.gpsimd.tensor_scalar(
                out=tab[:, :, 0, :].rearrange("p h (r d) -> p h r d", d=DH),
                in0=sq[:].unsqueeze(2).to_broadcast([P, 2, reps, DH]),
                scalar1=-2.0,
                scalar2=1.0,
                op0=ALU.mult,
                op1=ALU.add,
            )
            nc.gpsimd.tensor_scalar(
                out=tab[:, :, 1, :].rearrange("p h (r d) -> p h r d", d=DH),
                in0=sswb[:].unsqueeze(2).to_broadcast([P, 2, reps, DH]),
                scalar1=1.0,
                scalar2=0.0,
                op0=ALU.mult,
                op1=ALU.add,
            )

        planes = {}
        inter = {}
        codes = {}
        acc = {}
        prod = {}
        res = {}

        def widen(c):
            n, g = divmod(c, PASSES)
            wd = TILES[n][1]
            pl = stage.tile([P, 4, wd], BF16, name="pl", tag="pl", bufs=5)
            for t in range(4):
                if (c < V_WIDENS and t < 2) or c in V_TAIL:
                    nc.vector.tensor_scalar(
                        out=pl[:, t, :],
                        in0=wb[c][:, t, :].bitcast(FP8),
                        scalar1=wsc[:, g, t : t + 1],
                        scalar2=None,
                        op0=ALU.mult,
                    )
                else:
                    nc.scalar.activation(
                        out=pl[:, t, :], in_=wb[c][:, t, :].bitcast(FP8), func=ACT.Copy, scale=wsc[:, g, t : t + 1]
                    )
            planes[c] = pl

        for c in range(V_WIDENS):
            widen(c)
        tables_s()

        xc = const.tile([P, PASSES, MT, P], U32, name="xc", align_bytes=64)
        xs = const.tile([P, PASSES, MT, P], U8, name="xs", align_bytes=64)
        xgs = {}

        def x_turn(mp, g):
            xt = psum.tile([P, 2, 2, P], F32, name="xt", tag="bank%d" % (3 * mp + g))
            for mi in range(2):
                words = x_sb[mp][:, mi, :].bitcast(F32)
                for u in range(2):
                    nc.tensor.transpose(xt[:, mi, u, :], words[:, 256 * g + u : 256 * (g + 1) : 2], ident[:])
            xg = stage.tile([P, 2 * P * 4], BF16, name="xg", tag="xg", bufs=6, align_bytes=64)
            nc.vector.tensor_copy(
                out=xg[:].bitcast(F32).rearrange("p (m r u) -> p m r u", m=2, u=2),
                in_=xt[:].rearrange("p m u r -> p m r u"),
            )
            xgs[(mp, g)] = xg

        def x_quant(mp, g):
            nc.vector.quantize_mx(
                out=xc[:, g, 2 * mp : 2 * mp + 2, :].rearrange("p m r -> p (m r)").bitcast(FP8X4),
                scales=xs[:, g, 2 * mp : 2 * mp + 2, :].rearrange("p m r -> p (m r)"),
                in_=xgs[(mp, g)][:],
            )


        def il_tile(c):
            if c not in inter:
                inter[c] = stage.tile([P, TILES[c // PASSES][1], 4], BF16, name="il", tag="il", bufs=5, align_bytes=64)
            return inter[c]

        def interleave(c):
            n = c // PASSES
            wd = TILES[n][1]
            vc = wd if c < V_WIDENS else VCOLS[n]
            pl = planes[c]
            il = il_tile(c)
            if c == G_CHUNK and G_COLS > 0:
                wd = wd - G_COLS
                vc = min(vc, wd)
            if vc > 0:
                nc.vector.tensor_copy(
                    out=il[:, 0:vc, :].rearrange("p (c i) t -> p c t i", i=8),
                    in_=pl[:, :, 0:vc].rearrange("p t (c i) -> p c t i", i=8),
                )
            if vc < wd:
                nc.scalar.copy(
                    out=il[:, vc:wd, :].rearrange("p (c i) t -> p c t i", i=8),
                    in_=pl[:, :, vc:wd].rearrange("p t (c i) -> p c t i", i=8),
                )
            inter[c] = il

        def g_interleave():
            il = il_tile(G_CHUNK)
            pl = planes[G_CHUNK]
            nc.gpsimd.tensor_copy(out=junku[:, 0:1], in_=codes[4][0][:, 0:1])
            nc.gpsimd.tensor_scalar(
                out=il[:, NB - G_COLS : NB, :].rearrange("p (c i) t -> p c t i", i=8),
                in0=pl[:, :, NB - G_COLS : NB].rearrange("p t (c i) -> p c t i", i=8),
                scalar1=1.0,
                scalar2=0.0,
                op0=ALU.mult,
                op1=ALU.add,
            )

        def quantize(c):
            wd = TILES[c // PASSES][1]
            wc = stage.tile([P, wd], U32, name="wc", tag="wc", bufs=4, align_bytes=64)
            ws = stage.tile([P, wd], U8, name="ws", tag="ws", bufs=4, align_bytes=64)
            nc.vector.quantize_mx(
                out=wc[:].bitcast(FP8X4), scales=ws[:], in_=inter[c][:].rearrange("p c t -> p (c t)")
            )
            codes[c] = (wc, ws)

        def matmuls(c):
            n, g = divmod(c, PASSES)
            wd = TILES[n][1]
            wc, ws = codes[c]
            for m in range(MT):
                if g == 0:
                    acc[(n, m)] = psum.tile([P, wd], F32, name="acc", tag="bank%d" % (4 * (n % 2) + m))
                nc.tensor.matmul_mx(
                    out=acc[(n, m)][:],
                    lhsT=xc[:, g, m, :].bitcast(FP8X4),
                    lhsT_scale=xs[:, g, m, :],
                    rhs=wc[:].bitcast(FP8X4),
                    rhs_scale=ws[:],
                    start=(g == 0),
                    stop=(g == PASSES - 1),
                )

        def result_tile(n):
            tens, lc = divmod(TILES[n][0], TCOLS)
            if lc == 0 and tens not in res:
                res[tens] = stage.tile([P, MT, TCOLS], F32, name="res", tag="res", bufs=2)
            return res[tens], lc

        def products(n, m):
            if m == 0:
                prod[n] = stage.tile([P, MT, 2, NB], F32, name="prod", tag="prod", bufs=2)
            off = TILES[n][0] % DH
            nc.vector.tensor_tensor(
                out=prod[n][:, m, :, :],
                in0=acc[(n, m)][:].unsqueeze(1).to_broadcast([P, 2, NB]),
                in1=tab[:, m % 2, :, off : off + NB],
                op=ALU.mult,
            )

        def sums(eng, n, m0, m1):
            r, lc = result_tile(n)
            rv = r[:, m0:m1, lc : lc + NB].rearrange("p m (g e i) -> p m g e i", e=2, i=16)
            cv = prod[n][:, m0:m1, 0, :].rearrange("p m (g e i) -> p m g e i", e=2, i=16)
            sv = prod[n][:, m0:m1, 1, :].rearrange("p m (g e i) -> p m g e i", e=2, i=16)
            for e in range(2):
                eng.tensor_tensor(out=rv[:, :, :, e, :], in0=cv[:, :, :, e, :], in1=sv[:, :, :, 1 - e, :], op=ALU.add)

        def store(n, m):
            r, lc = result_tile(n)
            tens = TILES[n][0] // TCOLS
            h0 = lc // DH
            h1 = (lc + TILES[n][1]) // DH
            b, e = divmod(m, 2)
            nc.sync.dma_start(
                out=outs[tens][b, h0:h1, :, :].rearrange("h (p e) d -> e p h d", e=2)[e],
                in_=r[:, m, DH * h0 : DH * h1].rearrange("p (h d) -> p h d", d=DH),
            )

        def evac(n, m):
            if "v" not in res:
                res["v"] = stage.tile([P, 2, HEADS, 2, DH], F32, name="res", tag="res", bufs=2)
            rv = res["v"]
            lc = TILES[n][0] % TCOLS
            wd = TILES[n][1]
            b, e = divmod(m, 2)
            eng_copy = nc.scalar.copy if m in S_EVAC[n - ROPED] else nc.vector.tensor_copy
            pos = lc
            while pos < lc + wd:
                h, d0 = divmod(pos, DH)
                if d0 == 0 and lc + wd - pos >= DH:
                    nh = (lc + wd - pos) // DH
                    eng_copy(
                        out=rv[:, b, h : h + nh, e, :],
                        in_=acc[(n, m)][:, pos - lc : pos - lc + DH * nh].rearrange("p (h d) -> p h d", d=DH),
                    )
                    pos += DH * nh
                else:
                    ln = min(DH - d0, lc + wd - pos)
                    eng_copy(out=rv[:, b, h, e, d0 : d0 + ln], in_=acc[(n, m)][:, pos - lc : pos - lc + ln])
                    pos += ln
            if e == 1:
                h0 = lc // DH
                h1 = (lc + wd) // DH
                nc.sync.dma_start(
                    out=outs[2][b, h0:h1, :, :].rearrange("h (p e) d -> p h (e d)", e=2),
                    in_=rv[:, b, h0:h1, :, :].rearrange("p h e d -> p h (e d)"),
                )

        def block(n):
            if 1 <= n < ROPED and GM > 0:
                sums(nc.vector, n - 1, GM, MT)
                r, lc = result_tile(n - 1)
                nc.gpsimd.tensor_copy(out=junk[:, 0:1], in_=r[:, MT - 1, lc + 16 : lc + 17])
                sums(nc.gpsimd, n - 1, 0, GM)
            if n == 0 and G_COLS > 0:
                g_interleave()
            if n < ROPED:
                for m in range(MT):
                    products(n, m)
                if n >= 1 and GM > 0:
                    for m in range(MT):
                        store(n - 1, m)
                if n == ROPED - 1 or GM == 0:
                    sums(nc.vector, n, 0, MT)
                    for m in range(MT):
                        store(n, m)

        for c in range(V_WIDENS):
            interleave(c)
        for c in range(V_WIDENS):
            quantize(c)
        tables_v()
        xorder = [(mp, g) for mp in range(2) for g in range(PASSES)]
        for mp, g in xorder:
            x_turn(mp, g)
        for mp, g in xorder:
            x_quant(mp, g)

        for k in range(NCH + 4):
            if V_WIDENS <= k < NCH:
                widen(k)
            if V_WIDENS <= k - 1 < NCH:
                interleave(k - 1)
            if 0 <= k - 2 < NCH:
                if k - 2 >= V_WIDENS:
                    quantize(k - 2)
                matmuls(k - 2)
            if (k - 1) % PASSES == PASSES - 1 and k > PASSES:
                block((k - 1) // PASSES - 1)
            for n in range(ROPED, NT):
                if k == min(PASSES * n + 6 + EVAC_LAG, NCH + 3 - (NT - 1 - n)):
                    for m in range(MT):
                        evac(n, m)
